import numpy as np
import ml_dtypes


def mxq(x, axis, fmt="e4m3"):
    dtype, down = {"e4m3": (ml_dtypes.float8_e4m3fn, 7), "e5m2": (ml_dtypes.float8_e5m2, 14)}[fmt]
    v = np.moveaxis(np.asarray(x, np.float32).astype(ml_dtypes.bfloat16).astype(np.float64), axis, -1)
    blocks = v.reshape(v.shape[:-1] + (-1, 32))
    amax = np.abs(blocks).max(-1, keepdims=True)
    byte = np.maximum(np.where(amax > 0, np.frexp(amax)[1] - 1 + 127, 0) - down, 1)
    scale = np.exp2(byte - 127.0)
    codes = (blocks / scale).astype(np.float32).astype(dtype).astype(np.float64)
    return np.moveaxis((codes * scale).reshape(v.shape), -1, axis)


WIDE = False


def mx_kscale(k):
    if not WIDE:
        return np.ones(k)
    levels = np.array([10, -10, 5, -5, 0])
    a = np.random.permutation(np.resize(levels, k // 512 * 4)).reshape(k // 512, 4)
    idx = np.arange(k)
    return np.exp2(a[idx // 512, idx % 128 // 32])


BF16 = ml_dtypes.bfloat16


def bf(x):
    return np.asarray(x, np.float32).astype(BF16)


def f64(x):
    return np.asarray(x).astype(np.float64)


B, C, NB, BW, T, EMB = 4, 2, 8, 128, 512, 128
F = NB * BW
FEAT = C * BW * 2
EPS = 1e-5


def setup_inputs():
    s = mx_kscale(FEAT)
    amp = np.exp2(np.random.uniform(-9.0, 1.0, (B, 1, 1, T)))
    return {"x_real": bf(amp * (np.random.standard_normal((B, C, F, T)) + 0.6)),
            "x_imag": bf(amp * (np.random.standard_normal((B, C, F, T)) + 0.2)),
            "ln_w": bf((1.0 + 0.1 * np.random.standard_normal((NB, FEAT))) * s),
            "ln_b": bf(0.1 * np.random.standard_normal((NB, FEAT)) * s),
            "fc_w": bf(np.random.standard_normal((NB, FEAT, EMB)) / np.sqrt(FEAT) / s[:, None]),
            "fc_b": bf(0.3 * np.random.standard_normal((NB, EMB)))}


def reference(x_real, x_imag, ln_w, ln_b, fc_w, fc_b):
    x_real, x_imag, ln_w, ln_b, fc_w, fc_b = f64(x_real), f64(x_imag), f64(ln_w), f64(ln_b), f64(fc_w), f64(fc_b)
    b, c, f, t = x_real.shape
    nb, feat = ln_w.shape
    bw = f // nb
    xr = np.transpose(x_real, (0, 3, 1, 2)).reshape(b, t, c, nb, bw)
    xi = np.transpose(x_imag, (0, 3, 1, 2)).reshape(b, t, c, nb, bw)
    xb = np.stack([xr, xi], axis=-1)
    xb = np.transpose(xb, (0, 3, 1, 2, 4, 5))
    xb = xb.reshape(b, nb, t, feat)
    mean = np.mean(xb, axis=-1, keepdims=True)
    var = np.mean(np.square(xb - mean), axis=-1, keepdims=True)
    xn = (xb - mean) * (1.0 / np.sqrt(var + EPS))
    xn = xn * ln_w[None, :, None, :] + ln_b[None, :, None, :]
    z = (mxq(xn, 3, "e4m3") @ mxq(fc_w, 1, "e4m3")[None]) + fc_b[None, :, None, :]
    return z

@@ -1,0 +1,236 @@
+from contextlib import ExitStack
+
+import concourse.mybir as mybir
+from concourse.masks import make_identity
+
+F32 = mybir.dt.float32
+BF16 = mybir.dt.bfloat16
+U32 = mybir.dt.uint32
+U8 = mybir.dt.uint8
+FP8X4 = mybir.dt.float8_e4m3fn_x4
+ACT = mybir.ActivationFunctionType
+ALU = mybir.AluOpType
+
+B, C, NB, BW, T, EMB = 4, 2, 8, 128, 512, 128
+P = 128
+SLOTS = 4
+EPS = 1e-5
+FLOPS = 2 * B * NB * T * (SLOTS * BW) * EMB
+GB = 4
+UNITS = B * NB
+GROUPS = UNITS // GB
+
+
+def tile_bandsplitmodule_kernel(tc, x_real, x_imag, ln_w, ln_b, fc_w, fc_b, out):
+    nc = tc.nc
+    with ExitStack() as ctx:
+        const = ctx.enter_context(tc.tile_pool(name="const", bufs=1))
+        xpool = ctx.enter_context(tc.tile_pool(name="xpool", bufs=4))
+        work = ctx.enter_context(tc.tile_pool(name="work", bufs=3))
+        small = ctx.enter_context(tc.tile_pool(name="small", bufs=6))
+        psx = ctx.enter_context(tc.psum_pool(name="psx", bufs=4))
+        psy = ctx.enter_context(tc.psum_pool(name="psy", bufs=3))
+        psz = ctx.enter_context(tc.psum_pool(name="psz", bufs=1))
+        ctx.enter_context(tc.manual_schedule())
+
+        xs, xts, mvs, sds, rstds, nmrs, ys, yts, xnps, grps, zos = {}, {}, {}, {}, {}, {}, {}, {}, {}, {}, {}
+        wq = {}
+
+        def load(grp_i):
+            b, g = grp_i // 2, grp_i % 2
+            xin = xpool.tile([P, SLOTS, GB, T], BF16, name="xin")
+            for c in range(C):
+                for r, src in enumerate((x_real, x_imag)):
+                    nc.sync.dma_start(
+                        out=xin[:, 2 * c + r, :, :],
+                        in_=src[b, c].rearrange("(n k) t -> k n t", k=BW)[:, GB * g : GB * g + GB, :],
+                    )
+            xs[grp_i] = xin
+
+        ident = const.tile([P, P], F32)
+        make_identity(nc, ident[:])
+        zero1 = const.tile([P, 1], F32)
+        nc.vector.memset(zero1[:], 0.0)
+        eps = const.tile([P, 1], F32)
+        nc.vector.tensor_scalar(out=eps[:], in0=zero1[:], scalar1=EPS, scalar2=None, op0=ALU.add)
+
+        lnraw = const.tile([P, 2 * BW], BF16)
+        nc.vector.memset(lnraw[:], 0.0)
+        nc.sync.dma_start(out=lnraw[0:16, :], in_=ln_w.rearrange("n (c q) -> (n c) q", c=C))
+        nc.sync.dma_start(out=lnraw[16:32, :], in_=ln_b.rearrange("n (c q) -> (n c) q", c=C))
+        load(0)
+        wraw = const.tile([P, NB, SLOTS, EMB], BF16)
+        nc.sync.dma_start(
+            out=wraw[:].rearrange("p n (c r) e -> p n c (r e)", c=C),
+            in_=fc_w.rearrange("n (c k r) e -> k n c (r e)", c=C, r=2),
+        )
+        load(1)
+        fcb = const.tile([P, NB * EMB], BF16)
+        nc.sync.dma_start(out=fcb[:], in_=fc_b.rearrange("n e -> (n e)").partition_broadcast(P))
+        load(2)
+
+        lnt = psx.tile([P, SLOTS, P], F32, tag="xt")
+        nc.tensor.transpose(lnt[:, 0, :], lnraw[:].bitcast(F32), ident[:])
+        lnv = lnt[:].bitcast(BF16)
+        lnw = const.tile([P, NB * SLOTS], F32)
+        lnb = const.tile([P, NB * SLOTS], F32)
+        nc.vector.tensor_copy(out=lnw[:], in_=lnv[:, 0, 0:32])
+        nc.vector.tensor_copy(out=lnb[:], in_=lnv[:, 0, 32:64])
+
+        def prep_weights():
+            wgrp = const.tile([P, NB, EMB, SLOTS], BF16, align_bytes=64)
+            nc.vector.tensor_copy(out=wgrp[:], in_=wraw[:].rearrange("p n s e -> p n e s"))
+            wcodes = const.tile([P, NB * EMB], U32, align_bytes=64)
+            wsc = const.tile([P, NB * EMB], U8, align_bytes=64)
+            nc.vector.quantize_mx(
+                out=wcodes[:].bitcast(FP8X4),
+                scales=wsc[:],
+                in_=wgrp[:].rearrange("p n e s -> p (n e s)"),
+            )
+            wq["codes"] = wcodes
+            wq["sc"] = wsc
+
+        def ok(u):
+            return 0 <= u < UNITS
+
+        def in_transposes(u):
+            xw = xs[u // GB][:].bitcast(F32)
+            j = u % GB
+            xts[u] = []
+            for h in range(2):
+                xt = psx.tile([P, SLOTS, P], F32, tag="xt")
+                for s in range(SLOTS):
+                    nc.tensor.transpose(xt[:, s, :], xw[:, s, j, P * h : P * h + P], ident[:])
+                xts[u].append(xt)
+
+        def stats(u):
+            mv = small.tile([P, 4, 2], F32, name="mv")
+            for h in range(2):
+                xb = xts[u][h][:].bitcast(BF16)
+                st = small.tile([P, 2, 6], F32, name="st")
+                for q in range(2):
+                    nc.vector.bn_stats(out=st[:, q, :], in_=xb[:, 2 * q : 2 * q + 2, :])
+                for e in range(2):
+                    nc.vector.bn_aggr(out=mv[:, 2 * h + e, :], in_=st[:, :, 3 * e : 3 * e + 3])
+            mvs[u] = mv
+
+        def root(u):
+            sd = small.tile([P, 4], F32, name="sd")
+            nc.scalar.activation(out=sd[:], in_=mvs[u][:, :, 1], func=ACT.Sqrt, bias=eps[:, 0:1], scale=1.0)
+            sds[u] = sd
+
+        def scalars(u):
+            rstd = small.tile([P, 4], F32, name="rstd")
+            nc.vector.reciprocal(out=rstd[:], in_=sds[u][:])
+            nmr = small.tile([P, 4], F32, name="nmr")
+            nc.vector.scalar_tensor_tensor(
+                out=nmr[:], in0=mvs[u][:, :, 0], scalar=-1.0, in1=rstd[:], op0=ALU.mult, op1=ALU.mult
+            )
+            rstds[u] = rstd
+            nmrs[u] = nmr
+
+        def normalise(u, he):
+            if he == 0:
+                ys[u] = work.tile([P, 4, SLOTS, BW], F32, name="y")
+            xv = xts[u][he // 2][:].bitcast(BF16).rearrange("p s (k e) -> p s k e", e=2)
+            nc.scalar.activation(
+                out=ys[u][:, he, :, :],
+                in_=xv[:, :, :, he % 2],
+                func=ACT.Identity,
+                scale=rstds[u][:, he : he + 1],
+                bias=nmrs[u][:, he : he + 1],
+            )
+
+        def back_transposes(u, s):
+            yt = psy.tile([P, T], F32, tag="yt")
+            for he in range(4):
+                nc.tensor.transpose(yt[:, P * he : P * he + P], ys[u][:, he, s, :], ident[:])
+            yts[(u, s)] = yt
+
+        def affine(u, s):
+            if s == 0:
+                xnps[u] = work.tile([P, SLOTS, T], BF16, name="xnp")
+            col = SLOTS * (u % NB) + s
+            nc.scalar.activation(
+                out=xnps[u][:, s, :],
+                in_=yts[(u, s)][:],
+                func=ACT.Identity,
+                scale=lnw[:, col : col + 1],
+                bias=lnb[:, col : col + 1],
+            )
+
+        def regroup(u):
+            grp = work.tile([P, T, SLOTS], BF16, align_bytes=64, name="grp")
+            nc.gpsimd.tensor_scalar(
+                out=grp[:].rearrange("p (c i) s -> p c s i", i=4),
+                in0=xnps[u][:].rearrange("p s (c i) -> p c s i", i=4),
+                scalar1=1.0,
+                scalar2=0.0,
+                op0=ALU.mult,
+                op1=ALU.add,
+            )
+            grps[u] = grp
+
+        def quantise_and_multiply(u):
+            n = u % NB
+            codes = work.tile([P, T], U32, align_bytes=64, name="codes")
+            sc = work.tile([P, T], U8, align_bytes=64, name="sc")
+            nc.vector.quantize_mx(
+                out=codes[:].bitcast(FP8X4), scales=sc[:], in_=grps[u][:].rearrange("p t s -> p (t s)")
+            )
+            zo = psz.tile([P, 4, EMB], F32, name="zo")
+            for he in range(4):
+                nc.tensor.matmul_mx(
+                    out=zo[:, he, :],
+                    lhsT=codes[:, P * he : P * he + P].bitcast(FP8X4),
+                    lhsT_scale=sc[:, P * he : P * he + P],
+                    rhs=wq["codes"][:, EMB * n : EMB * n + EMB].bitcast(FP8X4),
+                    rhs_scale=wq["sc"][:, EMB * n : EMB * n + EMB],
+                    start=True,
+                    stop=True,
+                )
+            zos[u] = zo
+
+        def finish(u):
+            b, n = u // NB, u % NB
+            zs = work.tile([P, 4, EMB], F32, name="zs")
+            nc.vector.tensor_tensor(
+                out=zs[:],
+                in0=zos[u][:],
+                in1=fcb[:, EMB * n : EMB * n + EMB].unsqueeze(1).to_broadcast([P, 4, EMB]),
+                op=ALU.add,
+            )
+            nc.sync.dma_start(
+                out=out[b, n].rearrange("(h p e) m -> p h (e m)", h=2, e=2),
+                in_=zs[:].rearrange("p (h e) m -> p h (e m)", h=2),
+            )
+
+        for i in range(-3, UNITS + 2):
+            if ok(i):
+                for s in range(3):
+                    back_transposes(i, s)
+            if ok(i + 1):
+                for he in range(3):
+                    normalise(i + 1, he)
+            if ok(i - 2):
+                quantise_and_multiply(i - 2)
+            if ok(i + 2):
+                root(i + 2)
+                scalars(i + 2)
+            if ok(i + 1):
+                normalise(i + 1, 3)
+            if ok(i - 2):
+                finish(i - 2)
+            if ok(i + 3):
+                in_transposes(i + 3)
+                stats(i + 3)
+                if (i + 3) % GB == 0 and (i + 3) // GB + 3 < GROUPS:
+                    load((i + 3) // GB + 3)
+            if i == -2:
+                prep_weights()
+            if ok(i):
+                affine(i, 0)
+                back_transposes(i, 3)
+                for s in range(1, SLOTS):
+                    affine(i, s)
+                regroup(i)

@@ -34,7 +34,7 @@ def tile_bandsplitmodule_kernel(tc, x_real, x_imag, ln_w, ln_b, fc_w, fc_b, out)
         ctx.enter_context(tc.manual_schedule())
 
         xs, xts, mvs, sds, rstds, nmrs, ys, yts, xnps, grps, zos = {}, {}, {}, {}, {}, {}, {}, {}, {}, {}, {}
-        wq = {}
+        wq, cds = {}, {}
 
         def load(grp_i):
             b, g = grp_i // 2, grp_i % 2
@@ -161,23 +161,23 @@ def tile_bandsplitmodule_kernel(tc, x_real, x_imag, ln_w, ln_b, fc_w, fc_b, out)
 
         def regroup(u):
             grp = work.tile([P, T, SLOTS], BF16, align_bytes=64, name="grp")
-            nc.gpsimd.tensor_scalar(
+            nc.vector.tensor_copy(
                 out=grp[:].rearrange("p (c i) s -> p c s i", i=4),
-                in0=xnps[u][:].rearrange("p s (c i) -> p c s i", i=4),
-                scalar1=1.0,
-                scalar2=0.0,
-                op0=ALU.mult,
-                op1=ALU.add,
+                in_=xnps[u][:].rearrange("p s (c i) -> p c s i", i=4),
             )
             grps[u] = grp
 
-        def quantise_and_multiply(u):
-            n = u % NB
+        def quantise(u):
             codes = work.tile([P, T], U32, align_bytes=64, name="codes")
             sc = work.tile([P, T], U8, align_bytes=64, name="sc")
             nc.vector.quantize_mx(
                 out=codes[:].bitcast(FP8X4), scales=sc[:], in_=grps[u][:].rearrange("p t s -> p (t s)")
             )
+            cds[u] = (codes, sc)
+
+        def multiply(u):
+            n = u % NB
+            codes, sc = cds[u]
             zo = psz.tile([P, 4, EMB], F32, name="zo")
             for he in range(4):
                 nc.tensor.matmul_mx(
@@ -209,20 +209,25 @@ def tile_bandsplitmodule_kernel(tc, x_real, x_imag, ln_w, ln_b, fc_w, fc_b, out)
             if ok(i):
                 for s in range(3):
                     back_transposes(i, s)
+            if ok(i - 1):
+                regroup(i - 1)
             if ok(i + 1):
                 for he in range(3):
                     normalise(i + 1, he)
             if ok(i - 2):
-                quantise_and_multiply(i - 2)
+                finish(i - 2)
+            if ok(i - 1):
+                quantise(i - 1)
             if ok(i + 2):
                 root(i + 2)
                 scalars(i + 2)
             if ok(i + 1):
                 normalise(i + 1, 3)
-            if ok(i - 2):
-                finish(i - 2)
             if ok(i + 3):
                 in_transposes(i + 3)
+            if ok(i - 1):
+                multiply(i - 1)
+            if ok(i + 3):
                 stats(i + 3)
                 if (i + 3) % GB == 0 and (i + 3) // GB + 3 < GROUPS:
                     load((i + 3) // GB + 3)
@@ -233,4 +238,3 @@ def tile_bandsplitmodule_kernel(tc, x_real, x_imag, ln_w, ln_b, fc_w, fc_b, out)
                 back_transposes(i, 3)
                 for s in range(1, SLOTS):
                     affine(i, s)
-                regroup(i)

@@ -27,14 +27,14 @@ def tile_bandsplitmodule_kernel(tc, x_real, x_imag, ln_w, ln_b, fc_w, fc_b, out)
         const = ctx.enter_context(tc.tile_pool(name="const", bufs=1))
         xpool = ctx.enter_context(tc.tile_pool(name="xpool", bufs=4))
         work = ctx.enter_context(tc.tile_pool(name="work", bufs=3))
-        small = ctx.enter_context(tc.tile_pool(name="small", bufs=6))
+        small = ctx.enter_context(tc.tile_pool(name="small", bufs=8))
         psx = ctx.enter_context(tc.psum_pool(name="psx", bufs=4))
         psy = ctx.enter_context(tc.psum_pool(name="psy", bufs=3))
         psz = ctx.enter_context(tc.psum_pool(name="psz", bufs=1))
         ctx.enter_context(tc.manual_schedule())
 
         xs, xts, mvs, sds, rstds, nmrs, ys, yts, xnps, grps, zos = {}, {}, {}, {}, {}, {}, {}, {}, {}, {}, {}
-        wq, cds = {}, {}
+        wq, cds, sts = {}, {}, {}
 
         def load(grp_i):
             b, g = grp_i // 2, grp_i % 2
@@ -93,46 +93,47 @@ def tile_bandsplitmodule_kernel(tc, x_real, x_imag, ln_w, ln_b, fc_w, fc_b, out)
         def ok(u):
             return 0 <= u < UNITS
 
-        def in_transposes(u):
+        def in_transposes(u, h):
             xw = xs[u // GB][:].bitcast(F32)
             j = u % GB
-            xts[u] = []
-            for h in range(2):
-                xt = psx.tile([P, SLOTS, P], F32, tag="xt")
-                for s in range(SLOTS):
-                    nc.tensor.transpose(xt[:, s, :], xw[:, s, j, P * h : P * h + P], ident[:])
-                xts[u].append(xt)
+            xt = psx.tile([P, SLOTS, P], F32, tag="xt")
+            for s in range(SLOTS):
+                nc.tensor.transpose(xt[:, s, :], xw[:, s, j, P * h : P * h + P], ident[:])
+            xts[(u, h)] = xt
 
-        def stats(u):
-            mv = small.tile([P, 4, 2], F32, name="mv")
-            for h in range(2):
-                xb = xts[u][h][:].bitcast(BF16)
-                st = small.tile([P, 2, 6], F32, name="st")
-                for q in range(2):
-                    nc.vector.bn_stats(out=st[:, q, :], in_=xb[:, 2 * q : 2 * q + 2, :])
-                for e in range(2):
-                    nc.vector.bn_aggr(out=mv[:, 2 * h + e, :], in_=st[:, :, 3 * e : 3 * e + 3])
-            mvs[u] = mv
+        def stats(u, h, q):
+            if q == 0:
+                sts[(u, h)] = small.tile([P, 2, 6], F32, name="st")
+            xb = xts[(u, h)][:].bitcast(BF16)
+            nc.vector.bn_stats(out=sts[(u, h)][:, q, :], in_=xb[:, 2 * q : 2 * q + 2, :])
+
+        def aggregate(u, h):
+            if h == 0:
+                mvs[u] = small.tile([P, 4, 2], F32, name="mv")
+            for e in range(2):
+                nc.vector.bn_aggr(out=mvs[u][:, 2 * h + e, :], in_=sts[(u, h)][:, :, 3 * e : 3 * e + 3])
 
         def root(u):
             sd = small.tile([P, 4], F32, name="sd")
             nc.scalar.activation(out=sd[:], in_=mvs[u][:, :, 1], func=ACT.Sqrt, bias=eps[:, 0:1], scale=1.0)
             sds[u] = sd
 
-        def scalars(u):
+        def inverse(u):
             rstd = small.tile([P, 4], F32, name="rstd")
             nc.vector.reciprocal(out=rstd[:], in_=sds[u][:])
+            rstds[u] = rstd
+
+        def shift(u):
             nmr = small.tile([P, 4], F32, name="nmr")
             nc.vector.scalar_tensor_tensor(
-                out=nmr[:], in0=mvs[u][:, :, 0], scalar=-1.0, in1=rstd[:], op0=ALU.mult, op1=ALU.mult
+                out=nmr[:], in0=mvs[u][:, :, 0], scalar=-1.0, in1=rstds[u][:], op0=ALU.mult, op1=ALU.mult
             )
-            rstds[u] = rstd
             nmrs[u] = nmr
 
         def normalise(u, he):
             if he == 0:
                 ys[u] = work.tile([P, 4, SLOTS, BW], F32, name="y")
-            xv = xts[u][he // 2][:].bitcast(BF16).rearrange("p s (k e) -> p s k e", e=2)
+            xv = xts[(u, he // 2)][:].bitcast(BF16).rearrange("p s (k e) -> p s k e", e=2)
             nc.scalar.activation(
                 out=ys[u][:, he, :, :],
                 in_=xv[:, :, :, he % 2],
@@ -161,10 +162,15 @@ def tile_bandsplitmodule_kernel(tc, x_real, x_imag, ln_w, ln_b, fc_w, fc_b, out)
 
         def regroup(u):
             grp = work.tile([P, T, SLOTS], BF16, align_bytes=64, name="grp")
-            nc.vector.tensor_copy(
-                out=grp[:].rearrange("p (c i) s -> p c s i", i=4),
-                in_=xnps[u][:].rearrange("p s (c i) -> p c s i", i=4),
-            )
+            for q in range(4):
+                nc.gpsimd.tensor_scalar(
+                    out=grp[:, P * q : P * q + P, :],
+                    in0=xnps[u][:, :, P * q : P * q + P].rearrange("p s t -> p t s"),
+                    scalar1=1.0,
+                    scalar2=0.0,
+                    op0=ALU.mult,
+                    op1=ALU.add,
+                )
             grps[u] = grp
 
         def quantise(u):
@@ -205,36 +211,57 @@ def tile_bandsplitmodule_kernel(tc, x_real, x_imag, ln_w, ln_b, fc_w, fc_b, out)
                 in_=zs[:].rearrange("p (h e) m -> p h (e m)", h=2),
             )
 
-        for i in range(-3, UNITS + 2):
-            if ok(i):
-                for s in range(3):
-                    back_transposes(i, s)
+        for i in range(-3, UNITS + 3):
+            if ok(i - 2):
+                quantise(i - 2)
             if ok(i - 1):
                 regroup(i - 1)
             if ok(i + 1):
-                for he in range(3):
-                    normalise(i + 1, he)
-            if ok(i - 2):
-                finish(i - 2)
-            if ok(i - 1):
-                quantise(i - 1)
-            if ok(i + 2):
-                root(i + 2)
-                scalars(i + 2)
-            if ok(i + 1):
-                normalise(i + 1, 3)
+                normalise(i + 1, 0)
+                normalise(i + 1, 1)
             if ok(i + 3):
-                in_transposes(i + 3)
-            if ok(i - 1):
-                multiply(i - 1)
-            if ok(i + 3):
-                stats(i + 3)
                 if (i + 3) % GB == 0 and (i + 3) // GB + 3 < GROUPS:
                     load((i + 3) // GB + 3)
+                in_transposes(i + 3, 0)
+            if ok(i):
+                affine(i, 0)
+                affine(i, 1)
+                back_transposes(i, 3)
+            if ok(i - 2):
+                multiply(i - 2)
+            if ok(i + 2):
+                root(i + 2)
+            if ok(i + 3):
+                stats(i + 3, 0, 0)
+            if ok(i + 2):
+                inverse(i + 2)
+            if ok(i + 3):
+                stats(i + 3, 0, 1)
+            if ok(i + 2):
+                shift(i + 2)
+            if ok(i + 3):
+                aggregate(i + 3, 0)
+            if ok(i + 1):
+                normalise(i + 1, 2)
+                normalise(i + 1, 3)
+            if ok(i + 3):
+                in_transposes(i + 3, 1)
+            if ok(i - 2):
+                finish(i - 2)
+            if ok(i + 1):
+                back_transposes(i + 1, 0)
+            if ok(i + 3):
+                stats(i + 3, 1, 0)
+                stats(i + 3, 1, 1)
+            if ok(i):
+                affine(i, 2)
+            if ok(i + 1):
+                back_transposes(i + 1, 1)
+            if ok(i + 3):
+                aggregate(i + 3, 1)
             if i == -2:
                 prep_weights()
             if ok(i):
-                affine(i, 0)
-                back_transposes(i, 3)
-                for s in range(1, SLOTS):
-                    affine(i, s)
+                affine(i, 3)
+            if ok(i + 1):
+                back_transposes(i + 1, 2)

@@ -19,6 +19,7 @@ FLOPS = 2 * B * NB * T * (SLOTS * BW) * EMB
 GB = 4
 UNITS = B * NB
 GROUPS = UNITS // GB
+WHOLE = ((0, GB),)
 
 
 def tile_bandsplitmodule_kernel(tc, x_real, x_imag, ln_w, ln_b, fc_w, fc_b, out):
@@ -36,15 +37,16 @@ def tile_bandsplitmodule_kernel(tc, x_real, x_imag, ln_w, ln_b, fc_w, fc_b, out)
         xs, xts, mvs, sds, rstds, nmrs, ys, yts, xnps, grps, zos = {}, {}, {}, {}, {}, {}, {}, {}, {}, {}, {}
         wq, cds, sts = {}, {}, {}
 
-        def load(grp_i):
+        def load(grp_i, cuts):
             b, g = grp_i // 2, grp_i % 2
             xin = xpool.tile([P, SLOTS, GB, T], BF16, name="xin")
-            for c in range(C):
-                for r, src in enumerate((x_real, x_imag)):
-                    nc.sync.dma_start(
-                        out=xin[:, 2 * c + r, :, :],
-                        in_=src[b, c].rearrange("(n k) t -> k n t", k=BW)[:, GB * g : GB * g + GB, :],
-                    )
+            for lo, hi in cuts:
+                for c in range(C):
+                    for r, src in enumerate((x_real, x_imag)):
+                        nc.sync.dma_start(
+                            out=xin[:, 2 * c + r, lo:hi, :],
+                            in_=src[b, c].rearrange("(n k) t -> k n t", k=BW)[:, GB * g + lo : GB * g + hi, :],
+                        )
             xs[grp_i] = xin
 
         ident = const.tile([P, P], F32)
@@ -56,18 +58,18 @@ def tile_bandsplitmodule_kernel(tc, x_real, x_imag, ln_w, ln_b, fc_w, fc_b, out)
 
         lnraw = const.tile([P, 2 * BW], BF16)
         nc.vector.memset(lnraw[:], 0.0)
-        nc.sync.dma_start(out=lnraw[0:16, :], in_=ln_w.rearrange("n (c q) -> (n c) q", c=C))
-        nc.sync.dma_start(out=lnraw[16:32, :], in_=ln_b.rearrange("n (c q) -> (n c) q", c=C))
-        load(0)
+        nc.scalar.dma_start(out=lnraw[0:16, :], in_=ln_w.rearrange("n (c q) -> (n c) q", c=C))
+        nc.scalar.dma_start(out=lnraw[16:32, :], in_=ln_b.rearrange("n (c q) -> (n c) q", c=C))
+        load(0, ((0, 1), (1, GB)))
         wraw = const.tile([P, NB, SLOTS, EMB], BF16)
         nc.sync.dma_start(
             out=wraw[:].rearrange("p n (c r) e -> p n c (r e)", c=C),
             in_=fc_w.rearrange("n (c k r) e -> k n c (r e)", c=C, r=2),
         )
-        load(1)
+        load(1, WHOLE)
         fcb = const.tile([P, NB * EMB], BF16)
         nc.sync.dma_start(out=fcb[:], in_=fc_b.rearrange("n e -> (n e)").partition_broadcast(P))
-        load(2)
+        load(2, WHOLE)
 
         lnt = psx.tile([P, SLOTS, P], F32, tag="xt")
         nc.tensor.transpose(lnt[:, 0, :], lnraw[:].bitcast(F32), ident[:])
@@ -148,21 +150,36 @@ def tile_bandsplitmodule_kernel(tc, x_real, x_imag, ln_w, ln_b, fc_w, fc_b, out)
                 nc.tensor.transpose(yt[:, P * he : P * he + P], ys[u][:, he, s, :], ident[:])
             yts[(u, s)] = yt
 
-        def affine(u, s):
-            if s == 0:
+        def affine(u, s, on_vector=False):
+            if u not in xnps:
                 xnps[u] = work.tile([P, SLOTS, T], BF16, name="xnp")
             col = SLOTS * (u % NB) + s
-            nc.scalar.activation(
-                out=xnps[u][:, s, :],
-                in_=yts[(u, s)][:],
-                func=ACT.Identity,
-                scale=lnw[:, col : col + 1],
-                bias=lnb[:, col : col + 1],
-            )
+            if on_vector:
+                nc.vector.tensor_scalar(
+                    out=xnps[u][:, s, :],
+                    in0=yts[(u, s)][:],
+                    scalar1=lnw[:, col : col + 1],
+                    scalar2=lnb[:, col : col + 1],
+                    op0=ALU.mult,
+                    op1=ALU.add,
+                )
+            else:
+                nc.scalar.activation(
+                    out=xnps[u][:, s, :],
+                    in_=yts[(u, s)][:],
+                    func=ACT.Identity,
+                    scale=lnw[:, col : col + 1],
+                    bias=lnb[:, col : col + 1],
+                )
 
         def regroup(u):
             grp = work.tile([P, T, SLOTS], BF16, align_bytes=64, name="grp")
-            for q in range(4):
+            if u >= UNITS - 2:
+                nc.vector.tensor_copy(
+                    out=grp[:].rearrange("p (c i) s -> p c s i", i=4),
+                    in_=xnps[u][:].rearrange("p s (c i) -> p c s i", i=4),
+                )
+            for q in range(4 if u < UNITS - 2 else 0):
                 nc.gpsimd.tensor_scalar(
                     out=grp[:, P * q : P * q + P, :],
                     in0=xnps[u][:, :, P * q : P * q + P].rearrange("p s t -> p t s"),
@@ -216,12 +233,14 @@ def tile_bandsplitmodule_kernel(tc, x_real, x_imag, ln_w, ln_b, fc_w, fc_b, out)
                 quantise(i - 2)
             if ok(i - 1):
                 regroup(i - 1)
+            if ok(i) and i % 2 == 0:
+                affine(i, 2, on_vector=True)
             if ok(i + 1):
                 normalise(i + 1, 0)
                 normalise(i + 1, 1)
             if ok(i + 3):
                 if (i + 3) % GB == 0 and (i + 3) // GB + 3 < GROUPS:
-                    load((i + 3) // GB + 3)
+                    load((i + 3) // GB + 3, WHOLE)
                 in_transposes(i + 3, 0)
             if ok(i):
                 affine(i, 0)
@@ -253,7 +272,7 @@ def tile_bandsplitmodule_kernel(tc, x_real, x_imag, ln_w, ln_b, fc_w, fc_b, out)
             if ok(i + 3):
                 stats(i + 3, 1, 0)
                 stats(i + 3, 1, 1)
-            if ok(i):
+            if ok(i) and i % 2 == 1:
                 affine(i, 2)
             if ok(i + 1):
                 back_transposes(i + 1, 1)

@@ -198,10 +198,25 @@ def tile_bandsplitmodule_kernel(tc, x_real, x_imag, ln_w, ln_b, fc_w, fc_b, out)
             )
             cds[u] = (codes, sc)
 
+        def idle_passes(u, passes):
+            if u not in zos:
+                zos[u] = psz.tile([P, 4, EMB], F32, name="zo")
+            for k in range(passes):
+                nc.tensor.matmul_mx(
+                    out=zos[u][:].rearrange("p a e -> p (a e)"),
+                    lhsT=wq["codes"][:, 0:P].bitcast(FP8X4),
+                    lhsT_scale=wq["sc"][:, 0:P],
+                    rhs=wq["codes"][:, 0 : 4 * EMB].bitcast(FP8X4),
+                    rhs_scale=wq["sc"][:, 0 : 4 * EMB],
+                    start=True,
+                    stop=True,
+                )
+
         def multiply(u):
             n = u % NB
             codes, sc = cds[u]
-            zo = psz.tile([P, 4, EMB], F32, name="zo")
+            idle_passes(u, 1)
+            zo = zos[u]
             for he in range(4):
                 nc.tensor.matmul_mx(
                     out=zo[:, he, :],
@@ -212,7 +227,6 @@ def tile_bandsplitmodule_kernel(tc, x_real, x_imag, ln_w, ln_b, fc_w, fc_b, out)
                     start=True,
                     stop=True,
                 )
-            zos[u] = zo
 
         def finish(u):
             b, n = u // NB, u % NB
@@ -269,6 +283,8 @@ def tile_bandsplitmodule_kernel(tc, x_real, x_imag, ln_w, ln_b, fc_w, fc_b, out)
                 finish(i - 2)
             if ok(i + 1):
                 back_transposes(i + 1, 0)
+            if ok(i - 1):
+                idle_passes(i - 1, 2)
             if ok(i + 3):
                 stats(i + 3, 1, 0)
                 stats(i + 3, 1, 1)

@@ -20,13 +20,16 @@ GB = 4
 UNITS = B * NB
 GROUPS = UNITS // GB
 WHOLE = ((0, GB),)
+FIRST_BAND_ALONE = ((0, 1), (1, GB))
+QUARTERS = 4
+AHEAD = 3
 
 
 def tile_bandsplitmodule_kernel(tc, x_real, x_imag, ln_w, ln_b, fc_w, fc_b, out):
     nc = tc.nc
     with ExitStack() as ctx:
         const = ctx.enter_context(tc.tile_pool(name="const", bufs=1))
-        xpool = ctx.enter_context(tc.tile_pool(name="xpool", bufs=4))
+        xpool = ctx.enter_context(tc.tile_pool(name="xpool", bufs=AHEAD + 1))
         work = ctx.enter_context(tc.tile_pool(name="work", bufs=3))
         small = ctx.enter_context(tc.tile_pool(name="small", bufs=8))
         psx = ctx.enter_context(tc.psum_pool(name="psx", bufs=4))
@@ -60,7 +63,7 @@ def tile_bandsplitmodule_kernel(tc, x_real, x_imag, ln_w, ln_b, fc_w, fc_b, out)
         nc.vector.memset(lnraw[:], 0.0)
         nc.scalar.dma_start(out=lnraw[0:16, :], in_=ln_w.rearrange("n (c q) -> (n c) q", c=C))
         nc.scalar.dma_start(out=lnraw[16:32, :], in_=ln_b.rearrange("n (c q) -> (n c) q", c=C))
-        load(0, ((0, 1), (1, GB)))
+        load(0, FIRST_BAND_ALONE)
         wraw = const.tile([P, NB, SLOTS, EMB], BF16)
         nc.sync.dma_start(
             out=wraw[:].rearrange("p n (c r) e -> p n c (r e)", c=C),
@@ -79,9 +82,17 @@ def tile_bandsplitmodule_kernel(tc, x_real, x_imag, ln_w, ln_b, fc_w, fc_b, out)
         nc.vector.tensor_copy(out=lnw[:], in_=lnv[:, 0, 0:32])
         nc.vector.tensor_copy(out=lnb[:], in_=lnv[:, 0, 32:64])
 
-        def prep_weights():
-            wgrp = const.tile([P, NB, EMB, SLOTS], BF16, align_bytes=64)
-            nc.vector.tensor_copy(out=wgrp[:], in_=wraw[:].rearrange("p n s e -> p n e s"))
+        wgrp = const.tile([P, NB, EMB, SLOTS], BF16, align_bytes=64)
+        nc.gpsimd.tensor_scalar(
+            out=wgrp[:],
+            in0=wraw[:].rearrange("p n s e -> p n e s"),
+            scalar1=1.0,
+            scalar2=0.0,
+            op0=ALU.mult,
+            op1=ALU.add,
+        )
+
+        def quantise_weights():
             wcodes = const.tile([P, NB * EMB], U32, align_bytes=64)
             wsc = const.tile([P, NB * EMB], U8, align_bytes=64)
             nc.vector.quantize_mx(
@@ -111,22 +122,22 @@ def tile_bandsplitmodule_kernel(tc, x_real, x_imag, ln_w, ln_b, fc_w, fc_b, out)
 
         def aggregate(u, h):
             if h == 0:
-                mvs[u] = small.tile([P, 4, 2], F32, name="mv")
+                mvs[u] = small.tile([P, QUARTERS, 2], F32, name="mv")
             for e in range(2):
                 nc.vector.bn_aggr(out=mvs[u][:, 2 * h + e, :], in_=sts[(u, h)][:, :, 3 * e : 3 * e + 3])
 
         def root(u):
-            sd = small.tile([P, 4], F32, name="sd")
+            sd = small.tile([P, QUARTERS], F32, name="sd")
             nc.scalar.activation(out=sd[:], in_=mvs[u][:, :, 1], func=ACT.Sqrt, bias=eps[:, 0:1], scale=1.0)
             sds[u] = sd
 
         def inverse(u):
-            rstd = small.tile([P, 4], F32, name="rstd")
+            rstd = small.tile([P, QUARTERS], F32, name="rstd")
             nc.vector.reciprocal(out=rstd[:], in_=sds[u][:])
             rstds[u] = rstd
 
         def shift(u):
-            nmr = small.tile([P, 4], F32, name="nmr")
+            nmr = small.tile([P, QUARTERS], F32, name="nmr")
             nc.vector.scalar_tensor_tensor(
                 out=nmr[:], in0=mvs[u][:, :, 0], scalar=-1.0, in1=rstds[u][:], op0=ALU.mult, op1=ALU.mult
             )
@@ -134,7 +145,7 @@ def tile_bandsplitmodule_kernel(tc, x_real, x_imag, ln_w, ln_b, fc_w, fc_b, out)
 
         def normalise(u, he):
             if he == 0:
-                ys[u] = work.tile([P, 4, SLOTS, BW], F32, name="y")
+                ys[u] = work.tile([P, QUARTERS, SLOTS, BW], F32, name="y")
             xv = xts[(u, he // 2)][:].bitcast(BF16).rearrange("p s (k e) -> p s k e", e=2)
             nc.scalar.activation(
                 out=ys[u][:, he, :, :],
@@ -146,7 +157,7 @@ def tile_bandsplitmodule_kernel(tc, x_real, x_imag, ln_w, ln_b, fc_w, fc_b, out)
 
         def back_transposes(u, s):
             yt = psy.tile([P, T], F32, tag="yt")
-            for he in range(4):
+            for he in range(QUARTERS):
                 nc.tensor.transpose(yt[:, P * he : P * he + P], ys[u][:, he, s, :], ident[:])
             yts[(u, s)] = yt
 
@@ -179,15 +190,16 @@ def tile_bandsplitmodule_kernel(tc, x_real, x_imag, ln_w, ln_b, fc_w, fc_b, out)
                     out=grp[:].rearrange("p (c i) s -> p c s i", i=4),
                     in_=xnps[u][:].rearrange("p s (c i) -> p c s i", i=4),
                 )
-            for q in range(4 if u < UNITS - 2 else 0):
-                nc.gpsimd.tensor_scalar(
-                    out=grp[:, P * q : P * q + P, :],
-                    in0=xnps[u][:, :, P * q : P * q + P].rearrange("p s t -> p t s"),
-                    scalar1=1.0,
-                    scalar2=0.0,
-                    op0=ALU.mult,
-                    op1=ALU.add,
-                )
+            else:
+                for q in range(QUARTERS):
+                    nc.gpsimd.tensor_scalar(
+                        out=grp[:, P * q : P * q + P, :],
+                        in0=xnps[u][:, :, P * q : P * q + P].rearrange("p s t -> p t s"),
+                        scalar1=1.0,
+                        scalar2=0.0,
+                        op0=ALU.mult,
+                        op1=ALU.add,
+                    )
             grps[u] = grp
 
         def quantise(u):
@@ -198,26 +210,11 @@ def tile_bandsplitmodule_kernel(tc, x_real, x_imag, ln_w, ln_b, fc_w, fc_b, out)
             )
             cds[u] = (codes, sc)
 
-        def idle_passes(u, passes):
-            if u not in zos:
-                zos[u] = psz.tile([P, 4, EMB], F32, name="zo")
-            for k in range(passes):
-                nc.tensor.matmul_mx(
-                    out=zos[u][:].rearrange("p a e -> p (a e)"),
-                    lhsT=wq["codes"][:, 0:P].bitcast(FP8X4),
-                    lhsT_scale=wq["sc"][:, 0:P],
-                    rhs=wq["codes"][:, 0 : 4 * EMB].bitcast(FP8X4),
-                    rhs_scale=wq["sc"][:, 0 : 4 * EMB],
-                    start=True,
-                    stop=True,
-                )
-
         def multiply(u):
             n = u % NB
             codes, sc = cds[u]
-            idle_passes(u, 1)
-            zo = zos[u]
-            for he in range(4):
+            zo = psz.tile([P, QUARTERS, EMB], F32, name="zo")
+            for he in range(QUARTERS):
                 nc.tensor.matmul_mx(
                     out=zo[:, he, :],
                     lhsT=codes[:, P * he : P * he + P].bitcast(FP8X4),
@@ -227,14 +224,15 @@ def tile_bandsplitmodule_kernel(tc, x_real, x_imag, ln_w, ln_b, fc_w, fc_b, out)
                     start=True,
                     stop=True,
                 )
+            zos[u] = zo
 
         def finish(u):
             b, n = u // NB, u % NB
-            zs = work.tile([P, 4, EMB], F32, name="zs")
+            zs = work.tile([P, QUARTERS, EMB], F32, name="zs")
             nc.vector.tensor_tensor(
                 out=zs[:],
                 in0=zos[u][:],
-                in1=fcb[:, EMB * n : EMB * n + EMB].unsqueeze(1).to_broadcast([P, 4, EMB]),
+                in1=fcb[:, EMB * n : EMB * n + EMB].unsqueeze(1).to_broadcast([P, QUARTERS, EMB]),
                 op=ALU.add,
             )
             nc.sync.dma_start(
@@ -243,6 +241,8 @@ def tile_bandsplitmodule_kernel(tc, x_real, x_imag, ln_w, ln_b, fc_w, fc_b, out)
             )
 
         for i in range(-3, UNITS + 3):
+            if i == 1:
+                quantise_weights()
             if ok(i - 2):
                 quantise(i - 2)
             if ok(i - 1):
@@ -253,8 +253,8 @@ def tile_bandsplitmodule_kernel(tc, x_real, x_imag, ln_w, ln_b, fc_w, fc_b, out)
                 normalise(i + 1, 0)
                 normalise(i + 1, 1)
             if ok(i + 3):
-                if (i + 3) % GB == 0 and (i + 3) // GB + 3 < GROUPS:
-                    load((i + 3) // GB + 3, WHOLE)
+                if (i + 3) % GB == 0 and (i + 3) // GB + AHEAD < GROUPS:
+                    load((i + 3) // GB + AHEAD, WHOLE)
                 in_transposes(i + 3, 0)
             if ok(i):
                 affine(i, 0)
@@ -283,8 +283,6 @@ def tile_bandsplitmodule_kernel(tc, x_real, x_imag, ln_w, ln_b, fc_w, fc_b, out)
                 finish(i - 2)
             if ok(i + 1):
                 back_transposes(i + 1, 0)
-            if ok(i - 1):
-                idle_passes(i - 1, 2)
             if ok(i + 3):
                 stats(i + 3, 1, 0)
                 stats(i + 3, 1, 1)
@@ -294,8 +292,6 @@ def tile_bandsplitmodule_kernel(tc, x_real, x_imag, ln_w, ln_b, fc_w, fc_b, out)
                 back_transposes(i + 1, 1)
             if ok(i + 3):
                 aggregate(i + 3, 1)
-            if i == -2:
-                prep_weights()
             if ok(i):
                 affine(i, 3)
             if ok(i + 1):

from contextlib import ExitStack

import concourse.mybir as mybir
from concourse.masks import make_identity

F32 = mybir.dt.float32
BF16 = mybir.dt.bfloat16
U32 = mybir.dt.uint32
U8 = mybir.dt.uint8
FP8X4 = mybir.dt.float8_e4m3fn_x4
ACT = mybir.ActivationFunctionType
ALU = mybir.AluOpType

B, C, NB, BW, T, EMB = 4, 2, 8, 128, 512, 128
P = 128
SLOTS = 4
EPS = 1e-5
FLOPS = 2 * B * NB * T * (SLOTS * BW) * EMB
GB = 4
UNITS = B * NB
GROUPS = UNITS // GB
WHOLE = ((0, GB),)
FIRST_BAND_ALONE = ((0, 1), (1, GB))
QUARTERS = 4
AHEAD = 3


def tile_bandsplitmodule_kernel(tc, x_real, x_imag, ln_w, ln_b, fc_w, fc_b, out):
    nc = tc.nc
    with ExitStack() as ctx:
        const = ctx.enter_context(tc.tile_pool(name="const", bufs=1))
        xpool = ctx.enter_context(tc.tile_pool(name="xpool", bufs=AHEAD + 1))
        work = ctx.enter_context(tc.tile_pool(name="work", bufs=3))
        small = ctx.enter_context(tc.tile_pool(name="small", bufs=8))
        psx = ctx.enter_context(tc.psum_pool(name="psx", bufs=4))
        psy = ctx.enter_context(tc.psum_pool(name="psy", bufs=3))
        psz = ctx.enter_context(tc.psum_pool(name="psz", bufs=1))
        ctx.enter_context(tc.manual_schedule())

        xs, xts, mvs, sds, rstds, nmrs, ys, yts, xnps, grps, zos = {}, {}, {}, {}, {}, {}, {}, {}, {}, {}, {}
        wq, cds, sts = {}, {}, {}

        def load(grp_i, cuts):
            b, g = grp_i // 2, grp_i % 2
            xin = xpool.tile([P, SLOTS, GB, T], BF16, name="xin")
            for lo, hi in cuts:
                for c in range(C):
                    for r, src in enumerate((x_real, x_imag)):
                        nc.sync.dma_start(
                            out=xin[:, 2 * c + r, lo:hi, :],
                            in_=src[b, c].rearrange("(n k) t -> k n t", k=BW)[:, GB * g + lo : GB * g + hi, :],
                        )
            xs[grp_i] = xin

        ident = const.tile([P, P], F32)
        make_identity(nc, ident[:])
        zero1 = const.tile([P, 1], F32)
        nc.vector.memset(zero1[:], 0.0)
        eps = const.tile([P, 1], F32)
        nc.vector.tensor_scalar(out=eps[:], in0=zero1[:], scalar1=EPS, scalar2=None, op0=ALU.add)

        lnraw = const.tile([P, 2 * BW], BF16)
        nc.vector.memset(lnraw[:], 0.0)
        nc.scalar.dma_start(out=lnraw[0:16, :], in_=ln_w.rearrange("n (c q) -> (n c) q", c=C))
        nc.scalar.dma_start(out=lnraw[16:32, :], in_=ln_b.rearrange("n (c q) -> (n c) q", c=C))
        load(0, FIRST_BAND_ALONE)
        wraw = const.tile([P, NB, SLOTS, EMB], BF16)
        nc.sync.dma_start(
            out=wraw[:].rearrange("p n (c r) e -> p n c (r e)", c=C),
            in_=fc_w.rearrange("n (c k r) e -> k n c (r e)", c=C, r=2),
        )
        load(1, WHOLE)
        fcb = const.tile([P, NB * EMB], BF16)
        nc.sync.dma_start(out=fcb[:], in_=fc_b.rearrange("n e -> (n e)").partition_broadcast(P))
        load(2, WHOLE)

        lnt = psx.tile([P, SLOTS, P], F32, tag="xt")
        nc.tensor.transpose(lnt[:, 0, :], lnraw[:].bitcast(F32), ident[:])
        lnv = lnt[:].bitcast(BF16)
        lnw = const.tile([P, NB * SLOTS], F32)
        lnb = const.tile([P, NB * SLOTS], F32)
        nc.vector.tensor_copy(out=lnw[:], in_=lnv[:, 0, 0:32])
        nc.vector.tensor_copy(out=lnb[:], in_=lnv[:, 0, 32:64])

        wgrp = const.tile([P, NB, EMB, SLOTS], BF16, align_bytes=64)
        nc.gpsimd.tensor_scalar(
            out=wgrp[:],
            in0=wraw[:].rearrange("p n s e -> p n e s"),
            scalar1=1.0,
            scalar2=0.0,
            op0=ALU.mult,
            op1=ALU.add,
        )

        def quantise_weights():
            wcodes = const.tile([P, NB * EMB], U32, align_bytes=64)
            wsc = const.tile([P, NB * EMB], U8, align_bytes=64)
            nc.vector.quantize_mx(
                out=wcodes[:].bitcast(FP8X4),
                scales=wsc[:],
                in_=wgrp[:].rearrange("p n e s -> p (n e s)"),
            )
            wq["codes"] = wcodes
            wq["sc"] = wsc

        def ok(u):
            return 0 <= u < UNITS

        def in_transposes(u, h):
            xw = xs[u // GB][:].bitcast(F32)
            j = u % GB
            xt = psx.tile([P, SLOTS, P], F32, tag="xt")
            for s in range(SLOTS):
                nc.tensor.transpose(xt[:, s, :], xw[:, s, j, P * h : P * h + P], ident[:])
            xts[(u, h)] = xt

        def stats(u, h, q):
            if q == 0:
                sts[(u, h)] = small.tile([P, 2, 6], F32, name="st")
            xb = xts[(u, h)][:].bitcast(BF16)
            nc.vector.bn_stats(out=sts[(u, h)][:, q, :], in_=xb[:, 2 * q : 2 * q + 2, :])

        def aggregate(u, h):
            if h == 0:
                mvs[u] = small.tile([P, QUARTERS, 2], F32, name="mv")
            for e in range(2):
                nc.vector.bn_aggr(out=mvs[u][:, 2 * h + e, :], in_=sts[(u, h)][:, :, 3 * e : 3 * e + 3])

        def root(u):
            sd = small.tile([P, QUARTERS], F32, name="sd")
            nc.scalar.activation(out=sd[:], in_=mvs[u][:, :, 1], func=ACT.Sqrt, bias=eps[:, 0:1], scale=1.0)
            sds[u] = sd

        def inverse(u):
            rstd = small.tile([P, QUARTERS], F32, name="rstd")
            nc.vector.reciprocal(out=rstd[:], in_=sds[u][:])
            rstds[u] = rstd

        def shift(u):
            nmr = small.tile([P, QUARTERS], F32, name="nmr")
            nc.vector.scalar_tensor_tensor(
                out=nmr[:], in0=mvs[u][:, :, 0], scalar=-1.0, in1=rstds[u][:], op0=ALU.mult, op1=ALU.mult
            )
            nmrs[u] = nmr

        def normalise(u, he):
            if he == 0:
                ys[u] = work.tile([P, QUARTERS, SLOTS, BW], F32, name="y")
            xv = xts[(u, he // 2)][:].bitcast(BF16).rearrange("p s (k e) -> p s k e", e=2)
            nc.scalar.activation(
                out=ys[u][:, he, :, :],
                in_=xv[:, :, :, he % 2],
                func=ACT.Identity,
                scale=rstds[u][:, he : he + 1],
                bias=nmrs[u][:, he : he + 1],
            )

        def back_transposes(u, s):
            yt = psy.tile([P, T], F32, tag="yt")
            for he in range(QUARTERS):
                nc.tensor.transpose(yt[:, P * he : P * he + P], ys[u][:, he, s, :], ident[:])
            yts[(u, s)] = yt

        def affine(u, s, on_vector=False):
            if u not in xnps:
                xnps[u] = work.tile([P, SLOTS, T], BF16, name="xnp")
            col = SLOTS * (u % NB) + s
            if on_vector:
                nc.vector.tensor_scalar(
                    out=xnps[u][:, s, :],
                    in0=yts[(u, s)][:],
                    scalar1=lnw[:, col : col + 1],
                    scalar2=lnb[:, col : col + 1],
                    op0=ALU.mult,
                    op1=ALU.add,
                )
            else:
                nc.scalar.activation(
                    out=xnps[u][:, s, :],
                    in_=yts[(u, s)][:],
                    func=ACT.Identity,
                    scale=lnw[:, col : col + 1],
                    bias=lnb[:, col : col + 1],
                )

        def regroup(u):
            grp = work.tile([P, T, SLOTS], BF16, align_bytes=64, name="grp")
            if u >= UNITS - 2:
                nc.vector.tensor_copy(
                    out=grp[:].rearrange("p (c i) s -> p c s i", i=4),
                    in_=xnps[u][:].rearrange("p s (c i) -> p c s i", i=4),
                )
            else:
                for q in range(QUARTERS):
                    nc.gpsimd.tensor_scalar(
                        out=grp[:, P * q : P * q + P, :],
                        in0=xnps[u][:, :, P * q : P * q + P].rearrange("p s t -> p t s"),
                        scalar1=1.0,
                        scalar2=0.0,
                        op0=ALU.mult,
                        op1=ALU.add,
                    )
            grps[u] = grp

        def quantise(u):
            codes = work.tile([P, T], U32, align_bytes=64, name="codes")
            sc = work.tile([P, T], U8, align_bytes=64, name="sc")
            nc.vector.quantize_mx(
                out=codes[:].bitcast(FP8X4), scales=sc[:], in_=grps[u][:].rearrange("p t s -> p (t s)")
            )
            cds[u] = (codes, sc)

        def multiply(u):
            n = u % NB
            codes, sc = cds[u]
            zo = psz.tile([P, QUARTERS, EMB], F32, name="zo")
            for he in range(QUARTERS):
                nc.tensor.matmul_mx(
                    out=zo[:, he, :],
                    lhsT=codes[:, P * he : P * he + P].bitcast(FP8X4),
                    lhsT_scale=sc[:, P * he : P * he + P],
                    rhs=wq["codes"][:, EMB * n : EMB * n + EMB].bitcast(FP8X4),
                    rhs_scale=wq["sc"][:, EMB * n : EMB * n + EMB],
                    start=True,
                    stop=True,
                )
            zos[u] = zo

        def finish(u):
            b, n = u // NB, u % NB
            zs = work.tile([P, QUARTERS, EMB], F32, name="zs")
            nc.vector.tensor_tensor(
                out=zs[:],
                in0=zos[u][:],
                in1=fcb[:, EMB * n : EMB * n + EMB].unsqueeze(1).to_broadcast([P, QUARTERS, EMB]),
                op=ALU.add,
            )
            nc.sync.dma_start(
                out=out[b, n].rearrange("(h p e) m -> p h (e m)", h=2, e=2),
                in_=zs[:].rearrange("p (h e) m -> p h (e m)", h=2),
            )

        for i in range(-3, UNITS + 3):
            if i == 1:
                quantise_weights()
            if ok(i - 2):
                quantise(i - 2)
            if ok(i - 1):
                regroup(i - 1)
            if ok(i) and i % 2 == 0:
                affine(i, 2, on_vector=True)
            if ok(i + 1):
                normalise(i + 1, 0)
                normalise(i + 1, 1)
            if ok(i + 3):
                if (i + 3) % GB == 0 and (i + 3) // GB + AHEAD < GROUPS:
                    load((i + 3) // GB + AHEAD, WHOLE)
                in_transposes(i + 3, 0)
            if ok(i):
                affine(i, 0)
                affine(i, 1)
                back_transposes(i, 3)
            if ok(i - 2):
                multiply(i - 2)
            if ok(i + 2):
                root(i + 2)
            if ok(i + 3):
                stats(i + 3, 0, 0)
            if ok(i + 2):
                inverse(i + 2)
            if ok(i + 3):
                stats(i + 3, 0, 1)
            if ok(i + 2):
                shift(i + 2)
            if ok(i + 3):
                aggregate(i + 3, 0)
            if ok(i + 1):
                normalise(i + 1, 2)
                normalise(i + 1, 3)
            if ok(i + 3):
                in_transposes(i + 3, 1)
            if ok(i - 2):
                finish(i - 2)
            if ok(i + 1):
                back_transposes(i + 1, 0)
            if ok(i + 3):
                stats(i + 3, 1, 0)
                stats(i + 3, 1, 1)
            if ok(i) and i % 2 == 1:
                affine(i, 2)
            if ok(i + 1):
                back_transposes(i + 1, 1)
            if ok(i + 3):
                aggregate(i + 3, 1)
            if ok(i):
                affine(i, 3)
            if ok(i + 1):
                back_transposes(i + 1, 2)
